import numpy as np
import ml_dtypes


def mxq(x, axis, fmt="e4m3"):
    dtype, down = {"e4m3": (ml_dtypes.float8_e4m3fn, 7), "e5m2": (ml_dtypes.float8_e5m2, 14)}[fmt]
    v = np.moveaxis(np.asarray(x, np.float32).astype(ml_dtypes.bfloat16).astype(np.float64), axis, -1)
    blocks = v.reshape(v.shape[:-1] + (-1, 32))
    amax = np.abs(blocks).max(-1, keepdims=True)
    byte = np.maximum(np.where(amax > 0, np.frexp(amax)[1] - 1 + 127, 0) - down, 1)
    scale = np.exp2(byte - 127.0)
    codes = (blocks / scale).astype(np.float32).astype(dtype).astype(np.float64)
    return np.moveaxis((codes * scale).reshape(v.shape), -1, axis)


WIDE = False


def mx_kscale(k):
    if not WIDE:
        return np.ones(k)
    levels = np.array([10, -10, 5, -5, 0])
    a = np.random.permutation(np.resize(levels, k // 512 * 4)).reshape(k // 512, 4)
    idx = np.arange(k)
    return np.exp2(a[idx // 512, idx % 128 // 32])


BF16 = ml_dtypes.bfloat16


def bf(x):
    return np.asarray(x, np.float32).astype(BF16)


def f64(x):
    return np.asarray(x).astype(np.float64)


B, S, D, H = 1, 512, 512, 8
DH = D // H
DQ = D // 2
VD = 2 * D * H
LAYER_INDEX = 0
LAMBDA_INIT = 0.8


def softmax(s):
    e = np.exp(s - s.max(-1, keepdims=True))
    return e / e.sum(-1, keepdims=True)


def setup_inputs():
    r = np.random.standard_normal
    t = mx_kscale(VD)
    qs = np.sqrt(2.0 * np.sqrt(DH / DQ))
    m = np.sqrt(0.3 / DH)
    return {"q1": bf(r((B, S, DQ)) * qs), "q2": bf(r((B, S, DQ)) * qs),
            "k1": bf(r((B, S, DQ)) * qs), "k2": bf(r((B, S, DQ)) * qs),
            "v": bf(r((B, S, VD)) * t),
            "Wo": bf(r((VD, D)) / np.sqrt(VD) / t[:, None]), "bo": bf(r(D) * 0.1),
            "lq1": bf(m + 0.05 * r(DH)), "lk1": bf(m + 0.05 * r(DH)),
            "lq2": bf(m + 0.05 * r(DH)), "lk2": bf(-m + 0.05 * r(DH))}


def reference(q1, q2, k1, k2, v, Wo, bo, lq1, lk1, lq2, lk2):
    scale = 1.0 / np.sqrt(DH)
    attn1 = softmax(f64(q1) @ f64(k1).transpose(0, 2, 1) * scale)
    attn2 = softmax(f64(q2) @ f64(k2).transpose(0, 2, 1) * scale)
    lam = (np.exp(np.sum(f64(lq1) * f64(lk1))) - np.exp(np.sum(f64(lq2) * f64(lk2)))
           + (LAMBDA_INIT - 0.6 * np.exp(-0.3 * LAYER_INDEX)))
    diff_attn = attn1 - lam * attn2
    out = mxq(diff_attn, 2, "e4m3") @ mxq(f64(v), 1, "e4m3")
    return (mxq(out, 2, "e4m3") @ mxq(f64(Wo), 0, "e4m3")) + f64(bo)

@@ -1,0 +1,322 @@
+import math
+from contextlib import ExitStack
+
+import concourse.mybir as mybir
+from concourse.masks import make_identity
+
+F32 = mybir.dt.float32
+BF16 = mybir.dt.bfloat16
+U32 = mybir.dt.uint32
+U8 = mybir.dt.uint8
+FP8X4 = mybir.dt.float8_e4m3fn_x4
+ALU = mybir.AluOpType
+ACT = mybir.ActivationFunctionType
+AXIS_X = mybir.AxisListType.X
+
+P = 128
+PACK = 4
+K_PASS = P * PACK
+
+S = 512
+DQ = 256
+DH = 64
+VD = 8192
+D = 512
+SCORE_SCALE = 1.0 / math.sqrt(DH)
+LAMBDA_OFFSET = 0.8 - 0.6 * math.exp(-0.3 * 0)
+
+ROW_TILES = S // P
+DQ_TILES = DQ // P
+PASSES = VD // K_PASS
+WO_COLS_ON_VECTOR = D // 2
+V_AHEAD = 3
+WO_AHEAD = 2
+
+FLOPS = 2 * (2 * S * S * DQ) + 2 * S * S * VD + 2 * S * VD * D
+
+
+def regroup(copy, grouped, rows):
+    copy(
+        out=grouped.rearrange("p (c i) t -> p c t i", i=4),
+        in_=rows.rearrange("p t (c i) -> p c t i", i=4),
+    )
+
+
+def tile_differentialattention_pa_kernel(tc, q1, q2, k1, k2, v, Wo, bo, lq1, lk1, lq2, lk2, out):
+    nc = tc.nc
+    with ExitStack() as stack:
+        stack.enter_context(tc.manual_schedule())
+        resident = stack.enter_context(tc.tile_pool(name="resident", bufs=1))
+        small = stack.enter_context(tc.tile_pool(name="small", bufs=4))
+        soft = stack.enter_context(tc.tile_pool(name="soft", bufs=3))
+        grouped_pool = stack.enter_context(tc.tile_pool(name="grouped", bufs=2))
+        codes_pool = stack.enter_context(tc.tile_pool(name="codes", bufs=3))
+        psum = stack.enter_context(tc.psum_pool(name="psum", bufs=8))
+
+        identity = resident.tile([P, P], BF16)
+        make_identity(nc, identity[:])
+
+        lam_vecs = resident.tile([P, 4, DH], BF16)
+        for i, vec in enumerate((lq1, lq2, lk1, lk2)):
+            nc.scalar.dma_start(out=lam_vecs[:, i, :], in_=vec.partition_broadcast(P))
+
+        rows_of = {}
+
+        def load_rows(name, src):
+            rows = resident.tile([P, ROW_TILES, DQ], BF16, name="rows_" + name)
+            nc.sync.dma_start(
+                out=rows[:], in_=src.flatten_outer_dims().rearrange("(p a) d -> p a d", a=ROW_TILES)
+            )
+            rows_of[name] = rows
+
+        v_by_key = v.flatten_outer_dims().rearrange("(p t) w -> p t w", t=PACK)
+        wo_by_row = Wo.rearrange("(g t p) n -> p g t n", t=PACK, p=P)
+        v_raw = {}
+        wo_raw = {}
+
+        def load_v(g):
+            v_raw[g] = resident.tile([P, PACK, K_PASS], BF16, name="v_raw%d" % g)
+            nc.sync.dma_start(out=v_raw[g][:], in_=v_by_key[:, :, g * K_PASS : (g + 1) * K_PASS])
+
+        def load_wo(g):
+            wo_raw[g] = resident.tile([P, PACK, D], BF16, name="wo_raw%d" % g)
+            nc.sync.dma_start(out=wo_raw[g][:], in_=wo_by_row[:, g, :, :])
+
+        load_rows("q1", q1)
+        load_rows("k1", k1)
+        load_rows("q2", q2)
+        load_rows("k2", k2)
+        for g in range(PASSES):
+            load_v(g)
+            load_wo(g)
+        bias = resident.tile([P, D], BF16)
+        nc.sync.dma_start(out=bias[:], in_=bo.partition_broadcast(P))
+
+        lam_products = resident.tile([P, 2, DH], F32)
+        nc.vector.tensor_tensor(
+            out=lam_products[:], in0=lam_vecs[:, 0:2, :], in1=lam_vecs[:, 2:4, :], op=ALU.mult
+        )
+        lam_sums = resident.tile([P, 2], F32)
+        nc.vector.reduce_sum(out=lam_sums[:], in_=lam_products[:], axis=AXIS_X)
+        lam_exps = resident.tile([P, 2], F32)
+        nc.scalar.activation(out=lam_exps[:], in_=lam_sums[:], func=ACT.Exp)
+        lam = resident.tile([P, 1], F32)
+        nc.vector.scalar_tensor_tensor(
+            out=lam[:],
+            in0=lam_exps[:, 0:1],
+            scalar=LAMBDA_OFFSET,
+            in1=lam_exps[:, 1:2],
+            op0=ALU.add,
+            op1=ALU.subtract,
+        )
+
+        v_codes = {}
+        wo_grouped = {}
+        wo_codes = {}
+        o_banks = {}
+        o_grouped = {}
+        o_codes = {}
+
+        def quantise(grouped, kind):
+            codes = codes_pool.tile([P, K_PASS], U32, tag=kind + "_codes", align_bytes=64)
+            scales = codes_pool.tile([P, K_PASS], U8, tag=kind + "_scales", align_bytes=64)
+            nc.vector.quantize_mx(
+                out=codes[:].bitcast(FP8X4), scales=scales[:], in_=grouped[:].rearrange("p c t -> p (c t)")
+            )
+            return codes, scales
+
+        def regroup_v(g):
+            grouped = grouped_pool.tile([P, K_PASS, PACK], BF16, tag="v_grouped", align_bytes=64)
+            regroup(nc.vector.tensor_copy, grouped[:], v_raw[g][:])
+            return grouped
+
+        def regroup_wo_on_scalar(g):
+            wo_grouped[g] = grouped_pool.tile(
+                [P, D, PACK], BF16, tag="wo_grouped", name="wo_grouped", align_bytes=64
+            )
+            split = WO_COLS_ON_VECTOR
+            regroup(nc.scalar.copy, wo_grouped[g][:, split:, :], wo_raw[g][:, :, split:])
+
+        def regroup_wo_on_vector(g):
+            split = WO_COLS_ON_VECTOR
+            regroup(nc.vector.tensor_copy, wo_grouped[g][:, :split, :], wo_raw[g][:, :, :split])
+
+        def first_product(g, a):
+            codes, scales = v_codes[g]
+            bank = psum.tile([P, PACK, P], F32, tag="bank")
+            for t in range(PACK):
+                nc.tensor.matmul_mx(
+                    out=bank[:, t, :],
+                    lhsT=codes[:, t * P : (t + 1) * P].bitcast(FP8X4),
+                    lhsT_scale=scales[:, t * P : (t + 1) * P],
+                    rhs=d_codes[:, a * P : (a + 1) * P].bitcast(FP8X4),
+                    rhs_scale=d_scales[:, a * P : (a + 1) * P],
+                    start=True,
+                    stop=True,
+                )
+            o_banks[(g, a)] = bank
+
+        def round_o(g, a):
+            if a == 0:
+                o_grouped[g] = grouped_pool.tile(
+                    [P, S, PACK], BF16, tag="o_grouped", name="o_grouped", align_bytes=64
+                )
+            nc.scalar.copy(
+                out=o_grouped[g][:, a * P : (a + 1) * P, :],
+                in_=o_banks[(g, a)][:].rearrange("p t r -> p r t"),
+            )
+
+        def second_product(g):
+            lhs_codes, lhs_scales = o_codes[g]
+            rhs_codes, rhs_scales = wo_codes[g]
+            for a in range(ROW_TILES):
+                nc.tensor.matmul_mx(
+                    out=out_sums[a][:],
+                    lhsT=lhs_codes[:, a * P : (a + 1) * P].bitcast(FP8X4),
+                    lhsT_scale=lhs_scales[:, a * P : (a + 1) * P],
+                    rhs=rhs_codes[:].bitcast(FP8X4),
+                    rhs_scale=rhs_scales[:],
+                    start=(g == 0),
+                    stop=(g == PASSES - 1),
+                )
+
+        transposed = {}
+
+        def flip(name, copy):
+            flipped = psum.tile([P, DQ_TILES, S], BF16, tag="bank")
+            for h in range(DQ_TILES):
+                for a in range(ROW_TILES):
+                    nc.tensor.transpose(
+                        flipped[:, h, a * P : (a + 1) * P],
+                        rows_of[name][:, a, h * P : (h + 1) * P],
+                        identity[:],
+                    )
+            kept = resident.tile([P, DQ_TILES, S], BF16, name="transposed_" + name)
+            copy(out=kept[:], in_=flipped[:])
+            transposed[name] = kept
+
+        flip("q1", nc.scalar.copy)
+        flip("k1", nc.vector.tensor_copy)
+        v_codes[0] = quantise(regroup_v(0), "v")
+        flip("q2", nc.scalar.copy)
+        flip("k2", nc.vector.tensor_copy)
+        regroup_wo_on_scalar(0)
+
+        def multiply_scores(q_name, k_name, a):
+            scores = psum.tile([P, S], F32, tag="bank")
+            for h in range(DQ_TILES):
+                nc.tensor.matmul(
+                    out=scores[:],
+                    lhsT=transposed[q_name][:, h, a * P : (a + 1) * P],
+                    rhs=transposed[k_name][:, h, :],
+                    start=(h == 0),
+                    stop=(h == DQ_TILES - 1),
+                )
+            return scores
+
+        def softmax_numerator(q_name, scores):
+            row_max = small.tile([P, 1], F32, tag="row_max")
+            nc.vector.reduce_max(out=row_max[:], in_=scores[:], axis=AXIS_X)
+            shift = small.tile([P, 1], F32, tag="shift")
+            nc.vector.tensor_scalar_mul(out=shift[:], in0=row_max[:], scalar1=-SCORE_SCALE)
+            numerator = soft.tile([P, S], F32, tag="numerator_" + q_name)
+            row_sum = small.tile([P, 1], F32, tag="row_sum_" + q_name)
+            nc.scalar.activation(
+                out=numerator[:],
+                in_=scores[:],
+                func=ACT.Exp,
+                bias=shift[:],
+                scale=SCORE_SCALE,
+                accum_out=row_sum[:],
+            )
+            return numerator, row_sum
+
+        def weigh(row_sum1, numerator2, row_sum2):
+            weight1 = small.tile([P, 1], F32, tag="weight1")
+            nc.vector.reciprocal(out=weight1[:], in_=row_sum1[:])
+            inverse2 = small.tile([P, 1], F32, tag="inverse2")
+            nc.vector.reciprocal(out=inverse2[:], in_=row_sum2[:])
+            weight2 = small.tile([P, 1], F32, tag="weight2")
+            nc.vector.tensor_mul(out=weight2[:], in0=inverse2[:], in1=lam[:])
+            subtrahend = soft.tile([P, S], F32, tag="subtrahend")
+            nc.scalar.activation(out=subtrahend[:], in_=numerator2[:], func=ACT.Copy, scale=weight2[:])
+            return weight1, subtrahend
+
+        d_grouped = resident.tile([P, S, PACK], BF16, align_bytes=64)
+
+        def difference(a, numerator1, weight1, subtrahend):
+            d_rows = soft.tile([P, S], BF16, tag="d_rows")
+            nc.vector.scalar_tensor_tensor(
+                out=d_rows[:],
+                in0=numerator1[:],
+                scalar=weight1[:],
+                in1=subtrahend[:],
+                op0=ALU.mult,
+                op1=ALU.subtract,
+            )
+            d_flipped = psum.tile([P, PACK, P], BF16, tag="bank")
+            for t in range(PACK):
+                nc.tensor.transpose(d_flipped[:, t, :], d_rows[:, t * P : (t + 1) * P], identity[:])
+            nc.scalar.copy(
+                out=d_grouped[:, a * P : (a + 1) * P, :], in_=d_flipped[:].rearrange("p t r -> p r t")
+            )
+
+        scores1 = {}
+        scores2 = {}
+        for a in range(ROW_TILES):
+            scores1[a] = multiply_scores("q1", "k1", a)
+            scores2[a] = multiply_scores("q2", "k2", a)
+        first = {}
+        second = {}
+        weighed = {}
+        for i in range(ROW_TILES + 2):
+            if i < ROW_TILES:
+                first[i] = softmax_numerator("q1", scores1[i])
+                second[i] = softmax_numerator("q2", scores2[i])
+            if 1 <= i <= ROW_TILES:
+                weighed[i - 1] = weigh(first[i - 1][1], *second[i - 1])
+            if i >= 2:
+                difference(i - 2, first[i - 2][0], *weighed[i - 2])
+            if i >= ROW_TILES:
+                v_codes[i - ROW_TILES + 1] = quantise(regroup_v(i - ROW_TILES + 1), "v")
+        d_codes = resident.tile([P, S], U32, align_bytes=64)
+        d_scales = resident.tile([P, S], U8, align_bytes=64)
+        nc.vector.quantize_mx(
+            out=d_codes[:].bitcast(FP8X4),
+            scales=d_scales[:],
+            in_=d_grouped[:].rearrange("p r t -> p (r t)"),
+        )
+        regroup_wo_on_vector(0)
+        regroup_wo_on_scalar(1)
+        regroup_wo_on_vector(1)
+        wo_codes[0] = quantise(wo_grouped[0], "wo")
+
+        for a in range(ROW_TILES):
+            first_product(0, a)
+        out_sums = [psum.tile([P, D], F32, tag="bank", name="out_sum%d" % a) for a in range(ROW_TILES)]
+
+        for g in range(PASSES + 1):
+            if g >= 1:
+                o_codes[g - 1] = quantise(o_grouped[g - 1], "o")
+            if g + V_AHEAD < PASSES:
+                v_next = regroup_v(g + V_AHEAD)
+            if g + 1 < PASSES:
+                wo_codes[g + 1] = quantise(wo_grouped[g + 1], "wo")
+            if g < PASSES:
+                for a in range(ROW_TILES):
+                    round_o(g, a)
+                    if g + 1 < PASSES:
+                        first_product(g + 1, a)
+            if g + WO_AHEAD < PASSES:
+                regroup_wo_on_scalar(g + WO_AHEAD)
+                regroup_wo_on_vector(g + WO_AHEAD)
+            if g + V_AHEAD < PASSES:
+                v_codes[g + V_AHEAD] = quantise(v_next, "v")
+            if g >= 1:
+                second_product(g - 1)
+
+        out_by_tile = out.flatten_outer_dims().rearrange("(p a) n -> p a n", a=ROW_TILES)
+        result = resident.tile([P, ROW_TILES, D], F32)
+        for a in range(ROW_TILES):
+            nc.vector.tensor_tensor(out=result[:, a, :], in0=out_sums[a][:], in1=bias[:], op=ALU.add)
+            nc.sync.dma_start(out=out_by_tile[:, a, :], in_=result[:, a, :])

@@ -26,9 +26,11 @@ SCORE_SCALE = 1.0 / math.sqrt(DH)
 LAMBDA_OFFSET = 0.8 - 0.6 * math.exp(-0.3 * 0)
 
 ROW_TILES = S // P
-DQ_TILES = DQ // P
+PAIR = 2
 PASSES = VD // K_PASS
-WO_COLS_ON_VECTOR = D // 2
+WO_COLS_ON_VECTOR = 176
+WO_COLS_IN_SBUF = D // 2
+BANKS_BEFORE_SECOND_PRODUCT = 2
 V_AHEAD = 3
 WO_AHEAD = 2
 
@@ -55,6 +57,8 @@ def tile_differentialattention_pa_kernel(tc, q1, q2, k1, k2, v, Wo, bo, lq1, lk1
 
         identity = resident.tile([P, P], BF16)
         make_identity(nc, identity[:])
+        identity_words = resident.tile([P, P], F32)
+        make_identity(nc, identity_words[:])
 
         lam_vecs = resident.tile([P, 4, DH], BF16)
         for i, vec in enumerate((lq1, lq2, lk1, lk2)):
@@ -92,25 +96,35 @@ def tile_differentialattention_pa_kernel(tc, q1, q2, k1, k2, v, Wo, bo, lq1, lk1
         bias = resident.tile([P, D], BF16)
         nc.sync.dma_start(out=bias[:], in_=bo.partition_broadcast(P))
 
-        lam_products = resident.tile([P, 2, DH], F32)
-        nc.vector.tensor_tensor(
-            out=lam_products[:], in0=lam_vecs[:, 0:2, :], in1=lam_vecs[:, 2:4, :], op=ALU.mult
-        )
-        lam_sums = resident.tile([P, 2], F32)
-        nc.vector.reduce_sum(out=lam_sums[:], in_=lam_products[:], axis=AXIS_X)
+        zero = resident.tile([P, 1], F32)
+        nc.vector.memset(zero[:], 0.0)
+        one = resident.tile([P, 1], F32)
+        nc.scalar.activation(out=one[:], in_=zero[:], func=ACT.Exp)
+
         lam_exps = resident.tile([P, 2], F32)
-        nc.scalar.activation(out=lam_exps[:], in_=lam_sums[:], func=ACT.Exp)
         lam = resident.tile([P, 1], F32)
-        nc.vector.scalar_tensor_tensor(
-            out=lam[:],
-            in0=lam_exps[:, 0:1],
-            scalar=LAMBDA_OFFSET,
-            in1=lam_exps[:, 1:2],
-            op0=ALU.add,
-            op1=ALU.subtract,
-        )
+
+        def exponentiate_lam_sums():
+            lam_products = resident.tile([P, 2, DH], F32)
+            nc.vector.tensor_tensor(
+                out=lam_products[:], in0=lam_vecs[:, 0:2, :], in1=lam_vecs[:, 2:4, :], op=ALU.mult
+            )
+            lam_sums = resident.tile([P, 2], F32)
+            nc.vector.reduce_sum(out=lam_sums[:], in_=lam_products[:], axis=AXIS_X)
+            nc.scalar.activation(out=lam_exps[:], in_=lam_sums[:], func=ACT.Exp)
+
+        def combine_lam():
+            nc.vector.scalar_tensor_tensor(
+                out=lam[:],
+                in0=lam_exps[:, 0:1],
+                scalar=LAMBDA_OFFSET,
+                in1=lam_exps[:, 1:2],
+                op0=ALU.add,
+                op1=ALU.subtract,
+            )
 
         v_codes = {}
+        wo_banks = {}
         wo_grouped = {}
         wo_codes = {}
         o_banks = {}
@@ -130,16 +144,31 @@ def tile_differentialattention_pa_kernel(tc, q1, q2, k1, k2, v, Wo, bo, lq1, lk1
             regroup(nc.vector.tensor_copy, grouped[:], v_raw[g][:])
             return grouped
 
+        def regroup_wo_on_tensor(g):
+            bank = psum.tile([P, D - WO_COLS_IN_SBUF, PACK], BF16, tag="bank")
+            for first in range(0, D - WO_COLS_IN_SBUF, P):
+                nc.tensor.matmul(
+                    out=bank[:, first : first + P, :].rearrange("p c t -> p (c t)"),
+                    lhsT=identity[:],
+                    rhs=wo_raw[g][
+                        :, :, WO_COLS_IN_SBUF + first : WO_COLS_IN_SBUF + first + P
+                    ].rearrange("p t c -> p c t"),
+                    start=True,
+                    stop=True,
+                )
+            wo_banks[g] = bank
+
         def regroup_wo_on_scalar(g):
             wo_grouped[g] = grouped_pool.tile(
                 [P, D, PACK], BF16, tag="wo_grouped", name="wo_grouped", align_bytes=64
             )
-            split = WO_COLS_ON_VECTOR
-            regroup(nc.scalar.copy, wo_grouped[g][:, split:, :], wo_raw[g][:, :, split:])
+            nc.scalar.copy(out=wo_grouped[g][:, WO_COLS_IN_SBUF:, :], in_=wo_banks[g][:])
+            cols = slice(WO_COLS_ON_VECTOR, WO_COLS_IN_SBUF)
+            regroup(nc.scalar.copy, wo_grouped[g][:, cols, :], wo_raw[g][:, :, cols])
 
         def regroup_wo_on_vector(g):
-            split = WO_COLS_ON_VECTOR
-            regroup(nc.vector.tensor_copy, wo_grouped[g][:, :split, :], wo_raw[g][:, :, :split])
+            cols = slice(0, WO_COLS_ON_VECTOR)
+            regroup(nc.vector.tensor_copy, wo_grouped[g][:, cols, :], wo_raw[g][:, :, cols])
 
         def first_product(g, a):
             codes, scales = v_codes[g]
@@ -166,51 +195,59 @@ def tile_differentialattention_pa_kernel(tc, q1, q2, k1, k2, v, Wo, bo, lq1, lk1
                 in_=o_banks[(g, a)][:].rearrange("p t r -> p r t"),
             )
 
-        def second_product(g):
+        def quantise_o(g, first_tile, tiles):
+            if first_tile == 0:
+                codes = codes_pool.tile([P, S], U32, tag="o_codes", align_bytes=64)
+                scales = codes_pool.tile([P, S], U8, tag="o_scales", align_bytes=64)
+                o_codes[g] = (codes, scales)
+            codes, scales = o_codes[g]
+            queries = slice(first_tile * P, (first_tile + tiles) * P)
+            nc.vector.quantize_mx(
+                out=codes[:, queries].bitcast(FP8X4),
+                scales=scales[:, queries],
+                in_=o_grouped[g][:, queries, :].rearrange("p r t -> p (r t)"),
+            )
+
+        def second_product(g, a):
             lhs_codes, lhs_scales = o_codes[g]
             rhs_codes, rhs_scales = wo_codes[g]
-            for a in range(ROW_TILES):
-                nc.tensor.matmul_mx(
-                    out=out_sums[a][:],
-                    lhsT=lhs_codes[:, a * P : (a + 1) * P].bitcast(FP8X4),
-                    lhsT_scale=lhs_scales[:, a * P : (a + 1) * P],
-                    rhs=rhs_codes[:].bitcast(FP8X4),
-                    rhs_scale=rhs_scales[:],
-                    start=(g == 0),
-                    stop=(g == PASSES - 1),
-                )
+            nc.tensor.matmul_mx(
+                out=out_sums[a][:],
+                lhsT=lhs_codes[:, a * P : (a + 1) * P].bitcast(FP8X4),
+                lhsT_scale=lhs_scales[:, a * P : (a + 1) * P],
+                rhs=rhs_codes[:].bitcast(FP8X4),
+                rhs_scale=rhs_scales[:],
+                start=(g == 0),
+                stop=(g == PASSES - 1),
+            )
 
         transposed = {}
 
         def flip(name, copy):
-            flipped = psum.tile([P, DQ_TILES, S], BF16, tag="bank")
-            for h in range(DQ_TILES):
-                for a in range(ROW_TILES):
-                    nc.tensor.transpose(
-                        flipped[:, h, a * P : (a + 1) * P],
-                        rows_of[name][:, a, h * P : (h + 1) * P],
-                        identity[:],
-                    )
-            kept = resident.tile([P, DQ_TILES, S], BF16, name="transposed_" + name)
-            copy(out=kept[:], in_=flipped[:])
+            flipped = psum.tile([P, S], F32, tag="bank")
+            for a in range(ROW_TILES):
+                nc.tensor.transpose(
+                    flipped[:, a * P : (a + 1) * P], rows_of[name][:, a, :].bitcast(F32), identity_words[:]
+                )
+            kept = resident.tile([P, S, PAIR], BF16, name="transposed_" + name)
+            copy(out=kept[:].rearrange("p r e -> p (r e)"), in_=flipped[:].bitcast(BF16))
             transposed[name] = kept
 
         flip("q1", nc.scalar.copy)
         flip("k1", nc.vector.tensor_copy)
-        v_codes[0] = quantise(regroup_v(0), "v")
         flip("q2", nc.scalar.copy)
+        exponentiate_lam_sums()
         flip("k2", nc.vector.tensor_copy)
-        regroup_wo_on_scalar(0)
 
         def multiply_scores(q_name, k_name, a):
             scores = psum.tile([P, S], F32, tag="bank")
-            for h in range(DQ_TILES):
+            for e in range(PAIR):
                 nc.tensor.matmul(
                     out=scores[:],
-                    lhsT=transposed[q_name][:, h, a * P : (a + 1) * P],
-                    rhs=transposed[k_name][:, h, :],
-                    start=(h == 0),
-                    stop=(h == DQ_TILES - 1),
+                    lhsT=transposed[q_name][:, a * P : (a + 1) * P, e],
+                    rhs=transposed[k_name][:, :, e],
+                    start=(e == 0),
+                    stop=(e == PAIR - 1),
                 )
             return scores
 
@@ -273,12 +310,20 @@ def tile_differentialattention_pa_kernel(tc, q1, q2, k1, k2, v, Wo, bo, lq1, lk1
             if i < ROW_TILES:
                 first[i] = softmax_numerator("q1", scores1[i])
                 second[i] = softmax_numerator("q2", scores2[i])
+            if i == 1:
+                combine_lam()
             if 1 <= i <= ROW_TILES:
                 weighed[i - 1] = weigh(first[i - 1][1], *second[i - 1])
+            if i >= ROW_TILES:
+                v_next = regroup_v(i - ROW_TILES)
             if i >= 2:
                 difference(i - 2, first[i - 2][0], *weighed[i - 2])
             if i >= ROW_TILES:
-                v_codes[i - ROW_TILES + 1] = quantise(regroup_v(i - ROW_TILES + 1), "v")
+                v_codes[i - ROW_TILES] = quantise(v_next, "v")
+                regroup_wo_on_tensor(i - ROW_TILES)
+            if i == ROW_TILES + 1:
+                regroup_wo_on_scalar(0)
+        v_next = regroup_v(2)
         d_codes = resident.tile([P, S], U32, align_bytes=64)
         d_scales = resident.tile([P, S], U8, align_bytes=64)
         nc.vector.quantize_mx(
@@ -287,6 +332,7 @@ def tile_differentialattention_pa_kernel(tc, q1, q2, k1, k2, v, Wo, bo, lq1, lk1
             in_=d_grouped[:].rearrange("p r t -> p (r t)"),
         )
         regroup_wo_on_vector(0)
+        v_codes[2] = quantise(v_next, "v")
         regroup_wo_on_scalar(1)
         regroup_wo_on_vector(1)
         wo_codes[0] = quantise(wo_grouped[0], "wo")
@@ -295,28 +341,41 @@ def tile_differentialattention_pa_kernel(tc, q1, q2, k1, k2, v, Wo, bo, lq1, lk1
             first_product(0, a)
         out_sums = [psum.tile([P, D], F32, tag="bank", name="out_sum%d" % a) for a in range(ROW_TILES)]
 
-        for g in range(PASSES + 1):
+        for g in range(PASSES - 1):
             if g >= 1:
-                o_codes[g - 1] = quantise(o_grouped[g - 1], "o")
+                quantise_o(g - 1, 0, ROW_TILES)
             if g + V_AHEAD < PASSES:
                 v_next = regroup_v(g + V_AHEAD)
-            if g + 1 < PASSES:
-                wo_codes[g + 1] = quantise(wo_grouped[g + 1], "wo")
-            if g < PASSES:
-                for a in range(ROW_TILES):
-                    round_o(g, a)
-                    if g + 1 < PASSES:
-                        first_product(g + 1, a)
+            wo_codes[g + 1] = quantise(wo_grouped[g + 1], "wo")
+            for a in range(ROW_TILES):
+                round_o(g, a)
+                if a >= 1:
+                    first_product(g + 1, a - 1)
+                elif g + WO_AHEAD < PASSES:
+                    regroup_wo_on_tensor(g + WO_AHEAD)
+                if g >= 1 and a == BANKS_BEFORE_SECOND_PRODUCT:
+                    for b in range(ROW_TILES):
+                        second_product(g - 1, b)
             if g + WO_AHEAD < PASSES:
                 regroup_wo_on_scalar(g + WO_AHEAD)
                 regroup_wo_on_vector(g + WO_AHEAD)
+            first_product(g + 1, ROW_TILES - 1)
             if g + V_AHEAD < PASSES:
                 v_codes[g + V_AHEAD] = quantise(v_next, "v")
-            if g >= 1:
-                second_product(g - 1)
 
         out_by_tile = out.flatten_outer_dims().rearrange("(p a) n -> p a n", a=ROW_TILES)
         result = resident.tile([P, ROW_TILES, D], F32)
-        for a in range(ROW_TILES):
+
+        def finish(a):
             nc.vector.tensor_tensor(out=result[:, a, :], in0=out_sums[a][:], in1=bias[:], op=ALU.add)
             nc.sync.dma_start(out=out_by_tile[:, a, :], in_=result[:, a, :])
+
+        quantise_o(PASSES - 2, 0, ROW_TILES)
+        for a in range(ROW_TILES):
+            second_product(PASSES - 2, a)
+        for a in range(ROW_TILES):
+            round_o(PASSES - 1, a)
+            quantise_o(PASSES - 1, a, 1)
+            second_product(PASSES - 1, a)
+        for a in range(ROW_TILES):
+            finish(a)

@@ -28,10 +28,9 @@ LAMBDA_OFFSET = 0.8 - 0.6 * math.exp(-0.3 * 0)
 ROW_TILES = S // P
 PAIR = 2
 PASSES = VD // K_PASS
-WO_COLS_ON_VECTOR = 176
-WO_COLS_IN_SBUF = D // 2
+WO_COLS_ON_VECTOR = D // 2
 BANKS_BEFORE_SECOND_PRODUCT = 2
-V_AHEAD = 3
+V_AHEAD = 2
 WO_AHEAD = 2
 
 FLOPS = 2 * (2 * S * S * DQ) + 2 * S * S * VD + 2 * S * VD * D
@@ -124,7 +123,6 @@ def tile_differentialattention_pa_kernel(tc, q1, q2, k1, k2, v, Wo, bo, lq1, lk1
             )
 
         v_codes = {}
-        wo_banks = {}
         wo_grouped = {}
         wo_codes = {}
         o_banks = {}
@@ -144,31 +142,16 @@ def tile_differentialattention_pa_kernel(tc, q1, q2, k1, k2, v, Wo, bo, lq1, lk1
             regroup(nc.vector.tensor_copy, grouped[:], v_raw[g][:])
             return grouped
 
-        def regroup_wo_on_tensor(g):
-            bank = psum.tile([P, D - WO_COLS_IN_SBUF, PACK], BF16, tag="bank")
-            for first in range(0, D - WO_COLS_IN_SBUF, P):
-                nc.tensor.matmul(
-                    out=bank[:, first : first + P, :].rearrange("p c t -> p (c t)"),
-                    lhsT=identity[:],
-                    rhs=wo_raw[g][
-                        :, :, WO_COLS_IN_SBUF + first : WO_COLS_IN_SBUF + first + P
-                    ].rearrange("p t c -> p c t"),
-                    start=True,
-                    stop=True,
-                )
-            wo_banks[g] = bank
-
         def regroup_wo_on_scalar(g):
             wo_grouped[g] = grouped_pool.tile(
                 [P, D, PACK], BF16, tag="wo_grouped", name="wo_grouped", align_bytes=64
             )
-            nc.scalar.copy(out=wo_grouped[g][:, WO_COLS_IN_SBUF:, :], in_=wo_banks[g][:])
-            cols = slice(WO_COLS_ON_VECTOR, WO_COLS_IN_SBUF)
-            regroup(nc.scalar.copy, wo_grouped[g][:, cols, :], wo_raw[g][:, :, cols])
+            split = WO_COLS_ON_VECTOR
+            regroup(nc.scalar.copy, wo_grouped[g][:, split:, :], wo_raw[g][:, :, split:])
 
         def regroup_wo_on_vector(g):
-            cols = slice(0, WO_COLS_ON_VECTOR)
-            regroup(nc.vector.tensor_copy, wo_grouped[g][:, cols, :], wo_raw[g][:, :, cols])
+            split = WO_COLS_ON_VECTOR
+            regroup(nc.vector.tensor_copy, wo_grouped[g][:, :split, :], wo_raw[g][:, :, :split])
 
         def first_product(g, a):
             codes, scales = v_codes[g]
@@ -223,21 +206,26 @@ def tile_differentialattention_pa_kernel(tc, q1, q2, k1, k2, v, Wo, bo, lq1, lk1
 
         transposed = {}
 
-        def flip(name, copy):
+        def flip(name):
             flipped = psum.tile([P, S], F32, tag="bank")
             for a in range(ROW_TILES):
                 nc.tensor.transpose(
                     flipped[:, a * P : (a + 1) * P], rows_of[name][:, a, :].bitcast(F32), identity_words[:]
                 )
             kept = resident.tile([P, S, PAIR], BF16, name="transposed_" + name)
-            copy(out=kept[:].rearrange("p r e -> p (r e)"), in_=flipped[:].bitcast(BF16))
+            if name in ("q1", "q2"):
+                nc.scalar.mul(
+                    out=kept[:].rearrange("p r e -> p (r e)"), in_=flipped[:].bitcast(BF16), mul=SCORE_SCALE
+                )
+            else:
+                nc.vector.tensor_copy(out=kept[:].rearrange("p r e -> p (r e)"), in_=flipped[:].bitcast(BF16))
             transposed[name] = kept
 
-        flip("q1", nc.scalar.copy)
-        flip("k1", nc.vector.tensor_copy)
-        flip("q2", nc.scalar.copy)
+        flip("q1")
+        flip("k1")
+        flip("q2")
         exponentiate_lam_sums()
-        flip("k2", nc.vector.tensor_copy)
+        flip("k2")
 
         def multiply_scores(q_name, k_name, a):
             scores = psum.tile([P, S], F32, tag="bank")
@@ -251,33 +239,23 @@ def tile_differentialattention_pa_kernel(tc, q1, q2, k1, k2, v, Wo, bo, lq1, lk1
                 )
             return scores
 
-        def softmax_numerator(q_name, scores):
-            row_max = small.tile([P, 1], F32, tag="row_max")
-            nc.vector.reduce_max(out=row_max[:], in_=scores[:], axis=AXIS_X)
+        def softmax_numerator(q_name, scores, row_sum):
             shift = small.tile([P, 1], F32, tag="shift")
-            nc.vector.tensor_scalar_mul(out=shift[:], in0=row_max[:], scalar1=-SCORE_SCALE)
+            nc.vector.reduce_max(out=shift[:], in_=scores[:], axis=AXIS_X, negate=True)
             numerator = soft.tile([P, S], F32, tag="numerator_" + q_name)
-            row_sum = small.tile([P, 1], F32, tag="row_sum_" + q_name)
             nc.scalar.activation(
-                out=numerator[:],
-                in_=scores[:],
-                func=ACT.Exp,
-                bias=shift[:],
-                scale=SCORE_SCALE,
-                accum_out=row_sum[:],
+                out=numerator[:], in_=scores[:], func=ACT.Exp, bias=shift[:], accum_out=row_sum
             )
-            return numerator, row_sum
+            return numerator
 
-        def weigh(row_sum1, numerator2, row_sum2):
-            weight1 = small.tile([P, 1], F32, tag="weight1")
-            nc.vector.reciprocal(out=weight1[:], in_=row_sum1[:])
-            inverse2 = small.tile([P, 1], F32, tag="inverse2")
-            nc.vector.reciprocal(out=inverse2[:], in_=row_sum2[:])
+        def weigh(row_sums, numerator2):
+            inverses = small.tile([P, 2], F32, tag="inverses")
+            nc.vector.reciprocal(out=inverses[:], in_=row_sums[:])
             weight2 = small.tile([P, 1], F32, tag="weight2")
-            nc.vector.tensor_mul(out=weight2[:], in0=inverse2[:], in1=lam[:])
+            nc.vector.tensor_mul(out=weight2[:], in0=inverses[:, 1:2], in1=lam[:])
             subtrahend = soft.tile([P, S], F32, tag="subtrahend")
             nc.scalar.activation(out=subtrahend[:], in_=numerator2[:], func=ACT.Copy, scale=weight2[:])
-            return weight1, subtrahend
+            return inverses[:, 0:1], subtrahend
 
         d_grouped = resident.tile([P, S, PACK], BF16, align_bytes=64)
 
@@ -286,7 +264,7 @@ def tile_differentialattention_pa_kernel(tc, q1, q2, k1, k2, v, Wo, bo, lq1, lk1
             nc.vector.scalar_tensor_tensor(
                 out=d_rows[:],
                 in0=numerator1[:],
-                scalar=weight1[:],
+                scalar=weight1,
                 in1=subtrahend[:],
                 op0=ALU.mult,
                 op1=ALU.subtract,
@@ -305,25 +283,27 @@ def tile_differentialattention_pa_kernel(tc, q1, q2, k1, k2, v, Wo, bo, lq1, lk1
             scores2[a] = multiply_scores("q2", "k2", a)
         first = {}
         second = {}
+        row_sums = {}
         weighed = {}
         for i in range(ROW_TILES + 2):
             if i < ROW_TILES:
-                first[i] = softmax_numerator("q1", scores1[i])
-                second[i] = softmax_numerator("q2", scores2[i])
+                row_sums[i] = small.tile([P, 2], F32, tag="row_sums", name="row_sums")
+                first[i] = softmax_numerator("q1", scores1[i], row_sums[i][:, 0:1])
+                second[i] = softmax_numerator("q2", scores2[i], row_sums[i][:, 1:2])
             if i == 1:
                 combine_lam()
+            if i == ROW_TILES:
+                v_next = regroup_v(0)
             if 1 <= i <= ROW_TILES:
-                weighed[i - 1] = weigh(first[i - 1][1], *second[i - 1])
-            if i >= ROW_TILES:
-                v_next = regroup_v(i - ROW_TILES)
-            if i >= 2:
-                difference(i - 2, first[i - 2][0], *weighed[i - 2])
-            if i >= ROW_TILES:
-                v_codes[i - ROW_TILES] = quantise(v_next, "v")
-                regroup_wo_on_tensor(i - ROW_TILES)
+                weighed[i - 1] = weigh(row_sums[i - 1], second[i - 1])
             if i == ROW_TILES + 1:
+                regroup_wo_on_vector(0)
+            if i >= 2:
+                difference(i - 2, first[i - 2], *weighed[i - 2])
+            if i == ROW_TILES:
+                v_codes[0] = quantise(v_next, "v")
                 regroup_wo_on_scalar(0)
-        v_next = regroup_v(2)
+        v_next = regroup_v(1)
         d_codes = resident.tile([P, S], U32, align_bytes=64)
         d_scales = resident.tile([P, S], U8, align_bytes=64)
         nc.vector.quantize_mx(
@@ -331,11 +311,10 @@ def tile_differentialattention_pa_kernel(tc, q1, q2, k1, k2, v, Wo, bo, lq1, lk1
             scales=d_scales[:],
             in_=d_grouped[:].rearrange("p r t -> p (r t)"),
         )
-        regroup_wo_on_vector(0)
-        v_codes[2] = quantise(v_next, "v")
+        wo_codes[0] = quantise(wo_grouped[0], "wo")
+        v_codes[1] = quantise(v_next, "v")
         regroup_wo_on_scalar(1)
         regroup_wo_on_vector(1)
-        wo_codes[0] = quantise(wo_grouped[0], "wo")
 
         for a in range(ROW_TILES):
             first_product(0, a)
@@ -349,17 +328,13 @@ def tile_differentialattention_pa_kernel(tc, q1, q2, k1, k2, v, Wo, bo, lq1, lk1
             wo_codes[g + 1] = quantise(wo_grouped[g + 1], "wo")
             for a in range(ROW_TILES):
                 round_o(g, a)
-                if a >= 1:
-                    first_product(g + 1, a - 1)
-                elif g + WO_AHEAD < PASSES:
-                    regroup_wo_on_tensor(g + WO_AHEAD)
-                if g >= 1 and a == BANKS_BEFORE_SECOND_PRODUCT:
+                first_product(g + 1, a)
+                if g >= 1 and a == BANKS_BEFORE_SECOND_PRODUCT - 1:
                     for b in range(ROW_TILES):
                         second_product(g - 1, b)
             if g + WO_AHEAD < PASSES:
                 regroup_wo_on_scalar(g + WO_AHEAD)
                 regroup_wo_on_vector(g + WO_AHEAD)
-            first_product(g + 1, ROW_TILES - 1)
             if g + V_AHEAD < PASSES:
                 v_codes[g + V_AHEAD] = quantise(v_next, "v")
 

@@ -28,7 +28,8 @@ LAMBDA_OFFSET = 0.8 - 0.6 * math.exp(-0.3 * 0)
 ROW_TILES = S // P
 PAIR = 2
 PASSES = VD // K_PASS
-WO_COLS_ON_VECTOR = D // 2
+WO_COLS_ON_VECTOR = 224
+WO_COLS_IN_SBUF = D - P
 BANKS_BEFORE_SECOND_PRODUCT = 2
 V_AHEAD = 2
 WO_AHEAD = 2
@@ -123,6 +124,7 @@ def tile_differentialattention_pa_kernel(tc, q1, q2, k1, k2, v, Wo, bo, lq1, lk1
             )
 
         v_codes = {}
+        wo_banks = {}
         wo_grouped = {}
         wo_codes = {}
         o_banks = {}
@@ -142,16 +144,31 @@ def tile_differentialattention_pa_kernel(tc, q1, q2, k1, k2, v, Wo, bo, lq1, lk1
             regroup(nc.vector.tensor_copy, grouped[:], v_raw[g][:])
             return grouped
 
+        def regroup_wo_on_tensor(g):
+            bank = psum.tile([P, D - WO_COLS_IN_SBUF, PACK], BF16, tag="bank")
+            for first_col in range(0, D - WO_COLS_IN_SBUF, P):
+                nc.tensor.matmul(
+                    out=bank[:, first_col : first_col + P, :].rearrange("p c t -> p (c t)"),
+                    lhsT=identity[:],
+                    rhs=wo_raw[g][
+                        :, :, WO_COLS_IN_SBUF + first_col : WO_COLS_IN_SBUF + first_col + P
+                    ].rearrange("p t c -> p c t"),
+                    start=True,
+                    stop=True,
+                )
+            wo_banks[g] = bank
+
         def regroup_wo_on_scalar(g):
             wo_grouped[g] = grouped_pool.tile(
                 [P, D, PACK], BF16, tag="wo_grouped", name="wo_grouped", align_bytes=64
             )
-            split = WO_COLS_ON_VECTOR
-            regroup(nc.scalar.copy, wo_grouped[g][:, split:, :], wo_raw[g][:, :, split:])
+            nc.scalar.copy(out=wo_grouped[g][:, WO_COLS_IN_SBUF:, :], in_=wo_banks[g][:])
+            cols = slice(WO_COLS_ON_VECTOR, WO_COLS_IN_SBUF)
+            regroup(nc.scalar.copy, wo_grouped[g][:, cols, :], wo_raw[g][:, :, cols])
 
         def regroup_wo_on_vector(g):
-            split = WO_COLS_ON_VECTOR
-            regroup(nc.vector.tensor_copy, wo_grouped[g][:, :split, :], wo_raw[g][:, :, :split])
+            cols = slice(0, WO_COLS_ON_VECTOR)
+            regroup(nc.vector.tensor_copy, wo_grouped[g][:, cols, :], wo_raw[g][:, :, cols])
 
         def first_product(g, a):
             codes, scales = v_codes[g]
@@ -300,9 +317,12 @@ def tile_differentialattention_pa_kernel(tc, q1, q2, k1, k2, v, Wo, bo, lq1, lk1
                 regroup_wo_on_vector(0)
             if i >= 2:
                 difference(i - 2, first[i - 2], *weighed[i - 2])
+            if i == ROW_TILES - 1:
+                regroup_wo_on_tensor(0)
             if i == ROW_TILES:
                 v_codes[0] = quantise(v_next, "v")
                 regroup_wo_on_scalar(0)
+                regroup_wo_on_tensor(1)
         v_next = regroup_v(1)
         d_codes = resident.tile([P, S], U32, align_bytes=64)
         d_scales = resident.tile([P, S], U8, align_bytes=64)
@@ -328,13 +348,17 @@ def tile_differentialattention_pa_kernel(tc, q1, q2, k1, k2, v, Wo, bo, lq1, lk1
             wo_codes[g + 1] = quantise(wo_grouped[g + 1], "wo")
             for a in range(ROW_TILES):
                 round_o(g, a)
-                first_product(g + 1, a)
-                if g >= 1 and a == BANKS_BEFORE_SECOND_PRODUCT - 1:
+                if a >= 1:
+                    first_product(g + 1, a - 1)
+                elif g + WO_AHEAD < PASSES:
+                    regroup_wo_on_tensor(g + WO_AHEAD)
+                if g >= 1 and a == BANKS_BEFORE_SECOND_PRODUCT:
                     for b in range(ROW_TILES):
                         second_product(g - 1, b)
             if g + WO_AHEAD < PASSES:
                 regroup_wo_on_scalar(g + WO_AHEAD)
                 regroup_wo_on_vector(g + WO_AHEAD)
+            first_product(g + 1, ROW_TILES - 1)
             if g + V_AHEAD < PASSES:
                 v_codes[g + V_AHEAD] = quantise(v_next, "v")
 

@@ -28,7 +28,7 @@ LAMBDA_OFFSET = 0.8 - 0.6 * math.exp(-0.3 * 0)
 ROW_TILES = S // P
 PAIR = 2
 PASSES = VD // K_PASS
-WO_COLS_ON_VECTOR = 224
+WO_COLS_ON_VECTOR = 192
 WO_COLS_IN_SBUF = D - P
 BANKS_BEFORE_SECOND_PRODUCT = 2
 V_AHEAD = 2
@@ -162,7 +162,10 @@ def tile_differentialattention_pa_kernel(tc, q1, q2, k1, k2, v, Wo, bo, lq1, lk1
             wo_grouped[g] = grouped_pool.tile(
                 [P, D, PACK], BF16, tag="wo_grouped", name="wo_grouped", align_bytes=64
             )
-            nc.scalar.copy(out=wo_grouped[g][:, WO_COLS_IN_SBUF:, :], in_=wo_banks[g][:])
+            nc.scalar.copy(
+                out=wo_grouped[g][:, WO_COLS_IN_SBUF:, :].rearrange("p c t -> p (c t)").bitcast(F32),
+                in_=wo_banks[g][:].rearrange("p c t -> p (c t)").bitcast(F32),
+            )
             cols = slice(WO_COLS_ON_VECTOR, WO_COLS_IN_SBUF)
             regroup(nc.scalar.copy, wo_grouped[g][:, cols, :], wo_raw[g][:, :, cols])
 

import math
from contextlib import ExitStack

import concourse.mybir as mybir
from concourse.masks import make_identity

F32 = mybir.dt.float32
BF16 = mybir.dt.bfloat16
U32 = mybir.dt.uint32
U8 = mybir.dt.uint8
FP8X4 = mybir.dt.float8_e4m3fn_x4
ALU = mybir.AluOpType
ACT = mybir.ActivationFunctionType
AXIS_X = mybir.AxisListType.X

P = 128
PACK = 4
K_PASS = P * PACK

S = 512
DQ = 256
DH = 64
VD = 8192
D = 512
SCORE_SCALE = 1.0 / math.sqrt(DH)
LAMBDA_OFFSET = 0.8 - 0.6 * math.exp(-0.3 * 0)

ROW_TILES = S // P
PAIR = 2
PASSES = VD // K_PASS
WO_COLS_ON_VECTOR = 192
WO_COLS_IN_SBUF = D - P
BANKS_BEFORE_SECOND_PRODUCT = 2
V_AHEAD = 2
WO_AHEAD = 2

FLOPS = 2 * (2 * S * S * DQ) + 2 * S * S * VD + 2 * S * VD * D


def regroup(copy, grouped, rows):
    copy(
        out=grouped.rearrange("p (c i) t -> p c t i", i=4),
        in_=rows.rearrange("p t (c i) -> p c t i", i=4),
    )


def tile_differentialattention_pa_kernel(tc, q1, q2, k1, k2, v, Wo, bo, lq1, lk1, lq2, lk2, out):
    nc = tc.nc
    with ExitStack() as stack:
        stack.enter_context(tc.manual_schedule())
        resident = stack.enter_context(tc.tile_pool(name="resident", bufs=1))
        small = stack.enter_context(tc.tile_pool(name="small", bufs=4))
        soft = stack.enter_context(tc.tile_pool(name="soft", bufs=3))
        grouped_pool = stack.enter_context(tc.tile_pool(name="grouped", bufs=2))
        codes_pool = stack.enter_context(tc.tile_pool(name="codes", bufs=3))
        psum = stack.enter_context(tc.psum_pool(name="psum", bufs=8))

        identity = resident.tile([P, P], BF16)
        make_identity(nc, identity[:])
        identity_words = resident.tile([P, P], F32)
        make_identity(nc, identity_words[:])

        lam_vecs = resident.tile([P, 4, DH], BF16)
        for i, vec in enumerate((lq1, lq2, lk1, lk2)):
            nc.scalar.dma_start(out=lam_vecs[:, i, :], in_=vec.partition_broadcast(P))

        rows_of = {}

        def load_rows(name, src):
            rows = resident.tile([P, ROW_TILES, DQ], BF16, name="rows_" + name)
            nc.sync.dma_start(
                out=rows[:], in_=src.flatten_outer_dims().rearrange("(p a) d -> p a d", a=ROW_TILES)
            )
            rows_of[name] = rows

        v_by_key = v.flatten_outer_dims().rearrange("(p t) w -> p t w", t=PACK)
        wo_by_row = Wo.rearrange("(g t p) n -> p g t n", t=PACK, p=P)
        v_raw = {}
        wo_raw = {}

        def load_v(g):
            v_raw[g] = resident.tile([P, PACK, K_PASS], BF16, name="v_raw%d" % g)
            nc.sync.dma_start(out=v_raw[g][:], in_=v_by_key[:, :, g * K_PASS : (g + 1) * K_PASS])

        def load_wo(g):
            wo_raw[g] = resident.tile([P, PACK, D], BF16, name="wo_raw%d" % g)
            nc.sync.dma_start(out=wo_raw[g][:], in_=wo_by_row[:, g, :, :])

        load_rows("q1", q1)
        load_rows("k1", k1)
        load_rows("q2", q2)
        load_rows("k2", k2)
        for g in range(PASSES):
            load_v(g)
            load_wo(g)
        bias = resident.tile([P, D], BF16)
        nc.sync.dma_start(out=bias[:], in_=bo.partition_broadcast(P))

        zero = resident.tile([P, 1], F32)
        nc.vector.memset(zero[:], 0.0)
        one = resident.tile([P, 1], F32)
        nc.scalar.activation(out=one[:], in_=zero[:], func=ACT.Exp)

        lam_exps = resident.tile([P, 2], F32)
        lam = resident.tile([P, 1], F32)

        def exponentiate_lam_sums():
            lam_products = resident.tile([P, 2, DH], F32)
            nc.vector.tensor_tensor(
                out=lam_products[:], in0=lam_vecs[:, 0:2, :], in1=lam_vecs[:, 2:4, :], op=ALU.mult
            )
            lam_sums = resident.tile([P, 2], F32)
            nc.vector.reduce_sum(out=lam_sums[:], in_=lam_products[:], axis=AXIS_X)
            nc.scalar.activation(out=lam_exps[:], in_=lam_sums[:], func=ACT.Exp)

        def combine_lam():
            nc.vector.scalar_tensor_tensor(
                out=lam[:],
                in0=lam_exps[:, 0:1],
                scalar=LAMBDA_OFFSET,
                in1=lam_exps[:, 1:2],
                op0=ALU.add,
                op1=ALU.subtract,
            )

        v_codes = {}
        wo_banks = {}
        wo_grouped = {}
        wo_codes = {}
        o_banks = {}
        o_grouped = {}
        o_codes = {}

        def quantise(grouped, kind):
            codes = codes_pool.tile([P, K_PASS], U32, tag=kind + "_codes", align_bytes=64)
            scales = codes_pool.tile([P, K_PASS], U8, tag=kind + "_scales", align_bytes=64)
            nc.vector.quantize_mx(
                out=codes[:].bitcast(FP8X4), scales=scales[:], in_=grouped[:].rearrange("p c t -> p (c t)")
            )
            return codes, scales

        def regroup_v(g):
            grouped = grouped_pool.tile([P, K_PASS, PACK], BF16, tag="v_grouped", align_bytes=64)
            regroup(nc.vector.tensor_copy, grouped[:], v_raw[g][:])
            return grouped

        def regroup_wo_on_tensor(g):
            bank = psum.tile([P, D - WO_COLS_IN_SBUF, PACK], BF16, tag="bank")
            for first_col in range(0, D - WO_COLS_IN_SBUF, P):
                nc.tensor.matmul(
                    out=bank[:, first_col : first_col + P, :].rearrange("p c t -> p (c t)"),
                    lhsT=identity[:],
                    rhs=wo_raw[g][
                        :, :, WO_COLS_IN_SBUF + first_col : WO_COLS_IN_SBUF + first_col + P
                    ].rearrange("p t c -> p c t"),
                    start=True,
                    stop=True,
                )
            wo_banks[g] = bank

        def regroup_wo_on_scalar(g):
            wo_grouped[g] = grouped_pool.tile(
                [P, D, PACK], BF16, tag="wo_grouped", name="wo_grouped", align_bytes=64
            )
            nc.scalar.copy(
                out=wo_grouped[g][:, WO_COLS_IN_SBUF:, :].rearrange("p c t -> p (c t)").bitcast(F32),
                in_=wo_banks[g][:].rearrange("p c t -> p (c t)").bitcast(F32),
            )
            cols = slice(WO_COLS_ON_VECTOR, WO_COLS_IN_SBUF)
            regroup(nc.scalar.copy, wo_grouped[g][:, cols, :], wo_raw[g][:, :, cols])

        def regroup_wo_on_vector(g):
            cols = slice(0, WO_COLS_ON_VECTOR)
            regroup(nc.vector.tensor_copy, wo_grouped[g][:, cols, :], wo_raw[g][:, :, cols])

        def first_product(g, a):
            codes, scales = v_codes[g]
            bank = psum.tile([P, PACK, P], F32, tag="bank")
            for t in range(PACK):
                nc.tensor.matmul_mx(
                    out=bank[:, t, :],
                    lhsT=codes[:, t * P : (t + 1) * P].bitcast(FP8X4),
                    lhsT_scale=scales[:, t * P : (t + 1) * P],
                    rhs=d_codes[:, a * P : (a + 1) * P].bitcast(FP8X4),
                    rhs_scale=d_scales[:, a * P : (a + 1) * P],
                    start=True,
                    stop=True,
                )
            o_banks[(g, a)] = bank

        def round_o(g, a):
            if a == 0:
                o_grouped[g] = grouped_pool.tile(
                    [P, S, PACK], BF16, tag="o_grouped", name="o_grouped", align_bytes=64
                )
            nc.scalar.copy(
                out=o_grouped[g][:, a * P : (a + 1) * P, :],
                in_=o_banks[(g, a)][:].rearrange("p t r -> p r t"),
            )

        def quantise_o(g, first_tile, tiles):
            if first_tile == 0:
                codes = codes_pool.tile([P, S], U32, tag="o_codes", align_bytes=64)
                scales = codes_pool.tile([P, S], U8, tag="o_scales", align_bytes=64)
                o_codes[g] = (codes, scales)
            codes, scales = o_codes[g]
            queries = slice(first_tile * P, (first_tile + tiles) * P)
            nc.vector.quantize_mx(
                out=codes[:, queries].bitcast(FP8X4),
                scales=scales[:, queries],
                in_=o_grouped[g][:, queries, :].rearrange("p r t -> p (r t)"),
            )

        def second_product(g, a):
            lhs_codes, lhs_scales = o_codes[g]
            rhs_codes, rhs_scales = wo_codes[g]
            nc.tensor.matmul_mx(
                out=out_sums[a][:],
                lhsT=lhs_codes[:, a * P : (a + 1) * P].bitcast(FP8X4),
                lhsT_scale=lhs_scales[:, a * P : (a + 1) * P],
                rhs=rhs_codes[:].bitcast(FP8X4),
                rhs_scale=rhs_scales[:],
                start=(g == 0),
                stop=(g == PASSES - 1),
            )

        transposed = {}

        def flip(name):
            flipped = psum.tile([P, S], F32, tag="bank")
            for a in range(ROW_TILES):
                nc.tensor.transpose(
                    flipped[:, a * P : (a + 1) * P], rows_of[name][:, a, :].bitcast(F32), identity_words[:]
                )
            kept = resident.tile([P, S, PAIR], BF16, name="transposed_" + name)
            if name in ("q1", "q2"):
                nc.scalar.mul(
                    out=kept[:].rearrange("p r e -> p (r e)"), in_=flipped[:].bitcast(BF16), mul=SCORE_SCALE
                )
            else:
                nc.vector.tensor_copy(out=kept[:].rearrange("p r e -> p (r e)"), in_=flipped[:].bitcast(BF16))
            transposed[name] = kept

        flip("q1")
        flip("k1")
        flip("q2")
        exponentiate_lam_sums()
        flip("k2")

        def multiply_scores(q_name, k_name, a):
            scores = psum.tile([P, S], F32, tag="bank")
            for e in range(PAIR):
                nc.tensor.matmul(
                    out=scores[:],
                    lhsT=transposed[q_name][:, a * P : (a + 1) * P, e],
                    rhs=transposed[k_name][:, :, e],
                    start=(e == 0),
                    stop=(e == PAIR - 1),
                )
            return scores

        def softmax_numerator(q_name, scores, row_sum):
            shift = small.tile([P, 1], F32, tag="shift")
            nc.vector.reduce_max(out=shift[:], in_=scores[:], axis=AXIS_X, negate=True)
            numerator = soft.tile([P, S], F32, tag="numerator_" + q_name)
            nc.scalar.activation(
                out=numerator[:], in_=scores[:], func=ACT.Exp, bias=shift[:], accum_out=row_sum
            )
            return numerator

        def weigh(row_sums, numerator2):
            inverses = small.tile([P, 2], F32, tag="inverses")
            nc.vector.reciprocal(out=inverses[:], in_=row_sums[:])
            weight2 = small.tile([P, 1], F32, tag="weight2")
            nc.vector.tensor_mul(out=weight2[:], in0=inverses[:, 1:2], in1=lam[:])
            subtrahend = soft.tile([P, S], F32, tag="subtrahend")
            nc.scalar.activation(out=subtrahend[:], in_=numerator2[:], func=ACT.Copy, scale=weight2[:])
            return inverses[:, 0:1], subtrahend

        d_grouped = resident.tile([P, S, PACK], BF16, align_bytes=64)

        def difference(a, numerator1, weight1, subtrahend):
            d_rows = soft.tile([P, S], BF16, tag="d_rows")
            nc.vector.scalar_tensor_tensor(
                out=d_rows[:],
                in0=numerator1[:],
                scalar=weight1,
                in1=subtrahend[:],
                op0=ALU.mult,
                op1=ALU.subtract,
            )
            d_flipped = psum.tile([P, PACK, P], BF16, tag="bank")
            for t in range(PACK):
                nc.tensor.transpose(d_flipped[:, t, :], d_rows[:, t * P : (t + 1) * P], identity[:])
            nc.scalar.copy(
                out=d_grouped[:, a * P : (a + 1) * P, :], in_=d_flipped[:].rearrange("p t r -> p r t")
            )

        scores1 = {}
        scores2 = {}
        for a in range(ROW_TILES):
            scores1[a] = multiply_scores("q1", "k1", a)
            scores2[a] = multiply_scores("q2", "k2", a)
        first = {}
        second = {}
        row_sums = {}
        weighed = {}
        for i in range(ROW_TILES + 2):
            if i < ROW_TILES:
                row_sums[i] = small.tile([P, 2], F32, tag="row_sums", name="row_sums")
                first[i] = softmax_numerator("q1", scores1[i], row_sums[i][:, 0:1])
                second[i] = softmax_numerator("q2", scores2[i], row_sums[i][:, 1:2])
            if i == 1:
                combine_lam()
            if i == ROW_TILES:
                v_next = regroup_v(0)
            if 1 <= i <= ROW_TILES:
                weighed[i - 1] = weigh(row_sums[i - 1], second[i - 1])
            if i == ROW_TILES + 1:
                regroup_wo_on_vector(0)
            if i >= 2:
                difference(i - 2, first[i - 2], *weighed[i - 2])
            if i == ROW_TILES - 1:
                regroup_wo_on_tensor(0)
            if i == ROW_TILES:
                v_codes[0] = quantise(v_next, "v")
                regroup_wo_on_scalar(0)
                regroup_wo_on_tensor(1)
        v_next = regroup_v(1)
        d_codes = resident.tile([P, S], U32, align_bytes=64)
        d_scales = resident.tile([P, S], U8, align_bytes=64)
        nc.vector.quantize_mx(
            out=d_codes[:].bitcast(FP8X4),
            scales=d_scales[:],
            in_=d_grouped[:].rearrange("p r t -> p (r t)"),
        )
        wo_codes[0] = quantise(wo_grouped[0], "wo")
        v_codes[1] = quantise(v_next, "v")
        regroup_wo_on_scalar(1)
        regroup_wo_on_vector(1)

        for a in range(ROW_TILES):
            first_product(0, a)
        out_sums = [psum.tile([P, D], F32, tag="bank", name="out_sum%d" % a) for a in range(ROW_TILES)]

        for g in range(PASSES - 1):
            if g >= 1:
                quantise_o(g - 1, 0, ROW_TILES)
            if g + V_AHEAD < PASSES:
                v_next = regroup_v(g + V_AHEAD)
            wo_codes[g + 1] = quantise(wo_grouped[g + 1], "wo")
            for a in range(ROW_TILES):
                round_o(g, a)
                if a >= 1:
                    first_product(g + 1, a - 1)
                elif g + WO_AHEAD < PASSES:
                    regroup_wo_on_tensor(g + WO_AHEAD)
                if g >= 1 and a == BANKS_BEFORE_SECOND_PRODUCT:
                    for b in range(ROW_TILES):
                        second_product(g - 1, b)
            if g + WO_AHEAD < PASSES:
                regroup_wo_on_scalar(g + WO_AHEAD)
                regroup_wo_on_vector(g + WO_AHEAD)
            first_product(g + 1, ROW_TILES - 1)
            if g + V_AHEAD < PASSES:
                v_codes[g + V_AHEAD] = quantise(v_next, "v")

        out_by_tile = out.flatten_outer_dims().rearrange("(p a) n -> p a n", a=ROW_TILES)
        result = resident.tile([P, ROW_TILES, D], F32)

        def finish(a):
            nc.vector.tensor_tensor(out=result[:, a, :], in0=out_sums[a][:], in1=bias[:], op=ALU.add)
            nc.sync.dma_start(out=out_by_tile[:, a, :], in_=result[:, a, :])

        quantise_o(PASSES - 2, 0, ROW_TILES)
        for a in range(ROW_TILES):
            second_product(PASSES - 2, a)
        for a in range(ROW_TILES):
            round_o(PASSES - 1, a)
            quantise_o(PASSES - 1, a, 1)
            second_product(PASSES - 1, a)
        for a in range(ROW_TILES):
            finish(a)
